import numpy as np
import ml_dtypes


def mxq(x, axis, fmt="e4m3"):
    dtype, down = {"e4m3": (ml_dtypes.float8_e4m3fn, 7), "e5m2": (ml_dtypes.float8_e5m2, 14)}[fmt]
    v = np.moveaxis(np.asarray(x, np.float32).astype(ml_dtypes.bfloat16).astype(np.float64), axis, -1)
    blocks = v.reshape(v.shape[:-1] + (-1, 32))
    amax = np.abs(blocks).max(-1, keepdims=True)
    byte = np.maximum(np.where(amax > 0, np.frexp(amax)[1] - 1 + 127, 0) - down, 1)
    scale = np.exp2(byte - 127.0)
    codes = (blocks / scale).astype(np.float32).astype(dtype).astype(np.float64)
    return np.moveaxis((codes * scale).reshape(v.shape), -1, axis)


WIDE = False


def mx_kscale(k):
    if not WIDE:
        return np.ones(k)
    levels = np.array([10, -10, 5, -5, 0])
    a = np.random.permutation(np.resize(levels, k // 512 * 4)).reshape(k // 512, 4)
    idx = np.arange(k)
    return np.exp2(a[idx // 512, idx % 128 // 32])


BF16 = ml_dtypes.bfloat16


def bf(x):
    return np.asarray(x, np.float32).astype(BF16)


def f64(x):
    return np.asarray(x).astype(np.float64)


B, NH, T, D, N, CK = 1, 2, 8192, 256, 256, 512
KD = NH * N
EPS_LN = 1e-5
TARGET_ACTIVITY = 0.1


def layernorm(v):
    m = np.mean(v, axis=-1, keepdims=True)
    var = np.mean((v - m) ** 2, axis=-1, keepdims=True)
    return (v - m) / np.sqrt(var + EPS_LN)


def setup_inputs():
    t = mx_kscale(KD)
    xy = np.maximum(np.random.standard_normal((B, NH, T, N)) * 0.5, 0.0) * np.maximum(np.random.standard_normal((B, NH, T, N)), 0.0)
    return {'xy_sparse': bf(xy * t.reshape(NH, 1, N)),
            'decoder': bf(np.random.standard_normal((KD, D)) * 2.0 / np.sqrt(KD) / t[:, None]),
            'x': bf(np.random.standard_normal((B, 1, T, D))),
            'scale': bf(1.0 + 0.1 * np.random.standard_normal(D)),
            'running_activity': bf(TARGET_ACTIVITY * np.exp(0.5 * np.random.standard_normal(D)))}


def reference(xy_sparse, decoder, x, scale, running_activity):
    flat = f64(xy_sparse).transpose(0, 2, 1, 3).reshape(B, 1, T, KD)
    y_mlp = mxq(flat, 3, 'e4m3') @ mxq(f64(decoder), 0, 'e4m3')
    y = layernorm(y_mlp)
    regulation = TARGET_ACTIVITY / (f64(running_activity) + 1e-6)
    y = y * np.sqrt(regulation) * f64(scale)
    return layernorm(f64(x) + y)

@@ -1,0 +1,272 @@
+from contextlib import ExitStack
+
+import concourse.masks as masks
+import concourse.mybir as mybir
+
+F32 = mybir.dt.float32
+BF16 = mybir.dt.bfloat16
+U32 = mybir.dt.uint32
+U8 = mybir.dt.uint8
+FP8X4 = mybir.dt.float8_e4m3fn_x4
+ALU = mybir.AluOpType
+ACT = mybir.ActivationFunctionType
+
+P = 128
+HEADS = 2
+HEAD_DIM = 256
+K = HEADS * HEAD_DIM
+PACK = 4
+D = 256
+T = 8192
+TILES = 4
+BANK_TILES = 2
+BANKS = TILES // BANK_TILES
+GROUPS = T // (P * TILES)
+EPS_LN = 1e-5
+EPS_ACTIVITY = 1e-6
+TARGET_ACTIVITY = 0.1
+
+FLOPS = 2 * T * K * D
+
+
+def tile_bdhlayer_pc_t_kernel(tc, xy_sparse, decoder, x, scale, running_activity, out):
+    nc = tc.nc
+
+    xy_groups = xy_sparse[0].rearrange("h (g p j) n -> g p h (j n)", p=P, j=TILES)
+    x_groups = x.flatten_outer_dims().rearrange("(g p j) d -> g p (j d)", p=P, j=TILES)
+    out_groups = out.flatten_outer_dims().rearrange("(g p j) d -> g p (j d)", p=P, j=TILES)
+
+    with ExitStack() as ctx:
+        const = ctx.enter_context(tc.tile_pool(name="const", bufs=1))
+        inputs = ctx.enter_context(tc.tile_pool(name="inputs", bufs=GROUPS))
+        quant = ctx.enter_context(tc.tile_pool(name="quant", bufs=2))
+        work = ctx.enter_context(tc.tile_pool(name="work", bufs=3))
+        results = ctx.enter_context(tc.tile_pool(name="results", bufs=4))
+        stats = ctx.enter_context(tc.tile_pool(name="stats", bufs=3))
+        turned_pool = ctx.enter_context(tc.psum_pool(name="turned", bufs=2 * BANKS))
+        product_pool = ctx.enter_context(tc.psum_pool(name="product", bufs=2 * BANKS))
+        ctx.enter_context(tc.manual_schedule())
+
+        rows = const.tile([P, 2, D], BF16)
+        nc.vector.memset(rows[:], 0.0)
+        nc.scalar.dma_start(out=rows[0:1, 0, :], in_=scale.rearrange("(o d) -> o d", o=1))
+        nc.scalar.dma_start(out=rows[0:1, 1, :], in_=running_activity.rearrange("(o d) -> o d", o=1))
+        dec_raw = const.tile([P, PACK, D], BF16)
+        nc.sync.dma_start(
+            out=dec_raw[:].rearrange("p (h e) d -> p h (e d)", h=HEADS),
+            in_=decoder.rearrange("(h p e) d -> p h (e d)", h=HEADS, e=2),
+        )
+        xy_tiles = []
+        x_tiles = []
+        for g in range(GROUPS):
+            xy_sb = inputs.tile([P, HEADS, TILES * HEAD_DIM], BF16)
+            nc.sync.dma_start(out=xy_sb[:], in_=xy_groups[g])
+            xy_tiles.append(xy_sb)
+            x_sb = inputs.tile([P, TILES, D], BF16)
+            nc.sync.dma_start(out=x_sb[:].rearrange("p j d -> p (j d)"), in_=x_groups[g])
+            x_tiles.append(x_sb)
+
+        ident = const.tile([P, P], F32)
+        masks.make_identity(nc, ident[:])
+        ones = const.tile([P, P], BF16)
+        nc.vector.memset(ones[:], 1.0)
+        eps_ln = const.tile([P, 1], F32)
+        nc.vector.memset(eps_ln[:], EPS_LN)
+        eps_activity = const.tile([P, 1], F32)
+        nc.vector.memset(eps_activity[:], EPS_ACTIVITY / TARGET_ACTIVITY)
+
+        dec_grouped = const.tile([P, D, PACK], BF16, align_bytes=64)
+        nc.vector.tensor_copy(out=dec_grouped[:], in_=dec_raw[:].rearrange("p t d -> p d t"))
+        dec_codes = const.tile([P, D], U32, align_bytes=64)
+        dec_scales = const.tile([P, D], U8, align_bytes=64)
+        nc.vector.quantize_mx(
+            out=dec_codes[:].bitcast(FP8X4),
+            scales=dec_scales[:],
+            in_=dec_grouped[:].rearrange("p d t -> p (d t)"),
+        )
+
+        spread = product_pool.tile([P, BANK_TILES, D], F32, tag="product")
+        nc.tensor.matmul(
+            spread[:].rearrange("p a d -> p (a d)"),
+            lhsT=ones[:],
+            rhs=rows[:].rearrange("p a d -> p (a d)"),
+            start=True,
+            stop=True,
+        )
+        root = const.tile([P, D], F32)
+        nc.scalar.activation(
+            out=root[:], in_=spread[:, 1, :], func=ACT.Sqrt, scale=1.0 / TARGET_ACTIVITY, bias=eps_activity[:, 0:1]
+        )
+        regulation = const.tile([P, D], F32)
+        nc.vector.reciprocal(out=regulation[:], in_=root[:])
+        gain = const.tile([P, D], F32)
+        nc.vector.tensor_tensor(out=gain[:], in0=regulation[:], in1=spread[:, 0, :], op=ALU.mult)
+
+        turned_of = {}
+        grouped_of = {}
+        codes_of = {}
+        scales_of = {}
+        products_of = {}
+        mean_var_of = {}
+        deviation_of = {}
+        centred_of = {}
+        z_of = {}
+        z_sum_of = {}
+        square_sum_of = {}
+        deviation2_of = {}
+        rstd2_of = {}
+        shift_of = {}
+
+        def turn(g):
+            xy_words = xy_tiles[g][:].bitcast(F32).rearrange("p h (j w) -> p h j w", j=TILES)
+            turned_of[g] = []
+            for b in range(BANKS):
+                turned = turned_pool.tile([P, BANK_TILES, HEADS, P], F32)
+                turned_of[g].append(turned)
+                for a in range(BANK_TILES):
+                    for h in range(HEADS):
+                        nc.tensor.transpose(turned[:, a, h, :], xy_words[:, h, BANK_TILES * b + a, :], ident[:])
+
+        def regroup(g):
+            grouped = quant.tile([P, TILES * K], BF16, align_bytes=64)
+            grouped_of[g] = grouped
+            grouped_words = grouped[:].bitcast(F32).rearrange("p (j t h) -> p j t h", j=TILES, h=HEADS)
+            for b in range(BANKS):
+                nc.scalar.copy(
+                    out=grouped_words[:, BANK_TILES * b : BANK_TILES * (b + 1), :, :],
+                    in_=turned_of[g][b][:].rearrange("p a h t -> p a t h"),
+                )
+
+        def quantise(g):
+            codes = quant.tile([P, TILES * P], U32, align_bytes=64)
+            scales = quant.tile([P, TILES * P], U8, align_bytes=64)
+            codes_of[g] = codes
+            scales_of[g] = scales
+            nc.vector.quantize_mx(out=codes[:].bitcast(FP8X4), scales=scales[:], in_=grouped_of[g][:])
+
+        def multiply(g):
+            products_of[g] = []
+            for b in range(BANKS):
+                product = product_pool.tile([P, BANK_TILES, D], F32)
+                for a in range(BANK_TILES):
+                    tokens = slice(P * (BANK_TILES * b + a), P * (BANK_TILES * b + a + 1))
+                    nc.tensor.matmul_mx(
+                        out=product[:, a, :],
+                        lhsT=codes_of[g][:, tokens].bitcast(FP8X4),
+                        lhsT_scale=scales_of[g][:, tokens],
+                        rhs=dec_codes[:].bitcast(FP8X4),
+                        rhs_scale=dec_scales[:],
+                        start=True,
+                        stop=True,
+                    )
+                    products_of[g].append(product[:, a, :])
+
+        def first_moments(g):
+            moments = stats.tile([P, TILES, 6], F32)
+            mean_var = stats.tile([P, TILES, 2], F32)
+            mean_var_of[g] = mean_var
+            for j in range(TILES):
+                nc.vector.bn_stats(out=moments[:, j, :], in_=products_of[g][j])
+            for j in range(TILES):
+                nc.vector.bn_aggr(out=mean_var[:, j, :], in_=moments[:, j, :])
+
+        def first_root(g):
+            deviation = stats.tile([P, TILES], F32)
+            deviation_of[g] = deviation
+            nc.scalar.activation(out=deviation[:], in_=mean_var_of[g][:, :, 1], func=ACT.Sqrt, bias=eps_ln[:, 0:1])
+
+        def centre(g):
+            centred = work.tile([P, TILES, D], F32)
+            centred_of[g] = centred
+            for j in range(TILES):
+                nc.vector.scalar_tensor_tensor(
+                    out=centred[:, j, :],
+                    in0=products_of[g][j],
+                    scalar=mean_var_of[g][:, j, 0:1],
+                    in1=gain[:],
+                    op0=ALU.subtract,
+                    op1=ALU.mult,
+                )
+
+        def residual(g):
+            rstd = stats.tile([P, TILES], F32)
+            nc.vector.reciprocal(out=rstd[:], in_=deviation_of[g][:])
+            z = work.tile([P, TILES, D], F32)
+            z_sum = stats.tile([P, TILES], F32)
+            z_of[g] = z
+            z_sum_of[g] = z_sum
+            for j in range(TILES):
+                nc.vector.scalar_tensor_tensor(
+                    out=z[:, j, :],
+                    in0=centred_of[g][:, j, :],
+                    scalar=rstd[:, j : j + 1],
+                    in1=x_tiles[g][:, j, :],
+                    op0=ALU.mult,
+                    op1=ALU.add,
+                    accum_out=z_sum[:, j : j + 1],
+                )
+
+        def second_squares(g):
+            squares = work.tile([P, TILES, D], BF16)
+            square_sum = stats.tile([P, TILES], F32)
+            square_sum_of[g] = square_sum
+            for j in range(TILES):
+                nc.scalar.activation(
+                    out=squares[:, j, :],
+                    in_=z_of[g][:, j, :],
+                    func=ACT.Square,
+                    scale=-float(D),
+                    bias=z_sum_of[g][:, j : j + 1],
+                    accum_out=square_sum[:, j : j + 1],
+                )
+
+        def second_root(g):
+            deviation2 = stats.tile([P, TILES], F32)
+            deviation2_of[g] = deviation2
+            nc.scalar.activation(
+                out=deviation2[:],
+                in_=square_sum_of[g][:],
+                func=ACT.Sqrt,
+                scale=1.0 / float(D * D * D),
+                bias=eps_ln[:, 0:1],
+            )
+
+        def second_inverse(g):
+            rstd2 = stats.tile([P, TILES], F32)
+            rstd2_of[g] = rstd2
+            nc.vector.reciprocal(out=rstd2[:], in_=deviation2_of[g][:])
+            shift = stats.tile([P, TILES], F32)
+            shift_of[g] = shift
+            nc.vector.scalar_tensor_tensor(
+                out=shift[:], in0=z_sum_of[g][:], scalar=-1.0 / float(D), in1=rstd2[:], op0=ALU.mult, op1=ALU.mult
+            )
+
+        def finish(g):
+            result = results.tile([P, TILES, D], F32)
+            for j in range(TILES):
+                nc.scalar.activation(
+                    out=result[:, j, :],
+                    in_=z_of[g][:, j, :],
+                    func=ACT.Identity,
+                    scale=rstd2_of[g][:, j : j + 1],
+                    bias=shift_of[g][:, j : j + 1],
+                )
+            nc.sync.dma_start(out=out_groups[g], in_=result[:].rearrange("p j d -> p (j d)"))
+
+        def run(stage, g):
+            if 0 <= g < GROUPS:
+                stage(g)
+
+        for s in range(-3, GROUPS + 1):
+            run(quantise, s + 1)
+            run(multiply, s + 1)
+            run(turn, s + 3)
+            run(second_root, s - 1)
+            run(second_inverse, s - 1)
+            run(regroup, s + 2)
+            run(finish, s - 1)
+            run(first_moments, s)
+            run(first_root, s)
+            run(centre, s)
+            run(residual, s)
+            run(second_squares, s)

@@ -49,8 +49,8 @@ def tile_bdhlayer_pc_t_kernel(tc, xy_sparse, decoder, x, scale, running_activity
 
         rows = const.tile([P, 2, D], BF16)
         nc.vector.memset(rows[:], 0.0)
-        nc.scalar.dma_start(out=rows[0:1, 0, :], in_=scale.rearrange("(o d) -> o d", o=1))
-        nc.scalar.dma_start(out=rows[0:1, 1, :], in_=running_activity.rearrange("(o d) -> o d", o=1))
+        nc.sync.dma_start(out=rows[0:1, 0, :], in_=scale.rearrange("(o d) -> o d", o=1))
+        nc.sync.dma_start(out=rows[0:1, 1, :], in_=running_activity.rearrange("(o d) -> o d", o=1))
         dec_raw = const.tile([P, PACK, D], BF16)
         nc.sync.dma_start(
             out=dec_raw[:].rearrange("p (h e) d -> p h (e d)", h=HEADS),
@@ -93,12 +93,14 @@ def tile_bdhlayer_pc_t_kernel(tc, xy_sparse, decoder, x, scale, running_activity
             start=True,
             stop=True,
         )
-        root = const.tile([P, D], F32)
-        nc.scalar.activation(
-            out=root[:], in_=spread[:, 1, :], func=ACT.Sqrt, scale=1.0 / TARGET_ACTIVITY, bias=eps_activity[:, 0:1]
-        )
         regulation = const.tile([P, D], F32)
-        nc.vector.reciprocal(out=regulation[:], in_=root[:])
+        nc.scalar.activation(
+            out=regulation[:],
+            in_=spread[:, 1, :],
+            func=ACT.Abs_reciprocal_sqrt,
+            scale=1.0 / TARGET_ACTIVITY,
+            bias=eps_activity[:, 0:1],
+        )
         gain = const.tile([P, D], F32)
         nc.vector.tensor_tensor(out=gain[:], in0=regulation[:], in1=spread[:, 0, :], op=ALU.mult)
 
@@ -108,12 +110,11 @@ def tile_bdhlayer_pc_t_kernel(tc, xy_sparse, decoder, x, scale, running_activity
         scales_of = {}
         products_of = {}
         mean_var_of = {}
-        deviation_of = {}
+        rstd_of = {}
         centred_of = {}
         z_of = {}
         z_sum_of = {}
         square_sum_of = {}
-        deviation2_of = {}
         rstd2_of = {}
         shift_of = {}
 
@@ -127,33 +128,35 @@ def tile_bdhlayer_pc_t_kernel(tc, xy_sparse, decoder, x, scale, running_activity
                     for h in range(HEADS):
                         nc.tensor.transpose(turned[:, a, h, :], xy_words[:, h, BANK_TILES * b + a, :], ident[:])
 
-        def regroup(g):
-            grouped = quant.tile([P, TILES * K], BF16, align_bytes=64)
-            grouped_of[g] = grouped
-            grouped_words = grouped[:].bitcast(F32).rearrange("p (j t h) -> p j t h", j=TILES, h=HEADS)
-            for b in range(BANKS):
-                nc.scalar.copy(
-                    out=grouped_words[:, BANK_TILES * b : BANK_TILES * (b + 1), :, :],
-                    in_=turned_of[g][b][:].rearrange("p a h t -> p a t h"),
-                )
+        def regroup(g, b):
+            if b == 0:
+                grouped = quant.tile([P, BANKS, BANK_TILES * K], BF16, align_bytes=64)
+                grouped_of[g] = grouped
+            nc.scalar.copy(
+                out=grouped_of[g][:, b, :].bitcast(F32).rearrange("p (a t h) -> p a t h", a=BANK_TILES, h=HEADS),
+                in_=turned_of[g][b][:].rearrange("p a h t -> p a t h"),
+            )
 
         def quantise(g):
-            codes = quant.tile([P, TILES * P], U32, align_bytes=64)
-            scales = quant.tile([P, TILES * P], U8, align_bytes=64)
+            codes = quant.tile([P, BANKS, BANK_TILES * P], U32, align_bytes=64)
+            scales = quant.tile([P, BANKS, BANK_TILES * P], U8, align_bytes=64)
             codes_of[g] = codes
             scales_of[g] = scales
-            nc.vector.quantize_mx(out=codes[:].bitcast(FP8X4), scales=scales[:], in_=grouped_of[g][:])
+            for b in range(BANKS):
+                nc.vector.quantize_mx(
+                    out=codes[:, b, :].bitcast(FP8X4), scales=scales[:, b, :], in_=grouped_of[g][:, b, :]
+                )
 
         def multiply(g):
             products_of[g] = []
             for b in range(BANKS):
                 product = product_pool.tile([P, BANK_TILES, D], F32)
                 for a in range(BANK_TILES):
-                    tokens = slice(P * (BANK_TILES * b + a), P * (BANK_TILES * b + a + 1))
+                    tokens = slice(P * a, P * (a + 1))
                     nc.tensor.matmul_mx(
                         out=product[:, a, :],
-                        lhsT=codes_of[g][:, tokens].bitcast(FP8X4),
-                        lhsT_scale=scales_of[g][:, tokens],
+                        lhsT=codes_of[g][:, b, tokens].bitcast(FP8X4),
+                        lhsT_scale=scales_of[g][:, b, tokens],
                         rhs=dec_codes[:].bitcast(FP8X4),
                         rhs_scale=dec_scales[:],
                         start=True,
@@ -171,9 +174,11 @@ def tile_bdhlayer_pc_t_kernel(tc, xy_sparse, decoder, x, scale, running_activity
                 nc.vector.bn_aggr(out=mean_var[:, j, :], in_=moments[:, j, :])
 
         def first_root(g):
-            deviation = stats.tile([P, TILES], F32)
-            deviation_of[g] = deviation
-            nc.scalar.activation(out=deviation[:], in_=mean_var_of[g][:, :, 1], func=ACT.Sqrt, bias=eps_ln[:, 0:1])
+            rstd = stats.tile([P, TILES], F32)
+            rstd_of[g] = rstd
+            nc.scalar.activation(
+                out=rstd[:], in_=mean_var_of[g][:, :, 1], func=ACT.Abs_reciprocal_sqrt, bias=eps_ln[:, 0:1]
+            )
 
         def centre(g):
             centred = work.tile([P, TILES, D], F32)
@@ -189,8 +194,6 @@ def tile_bdhlayer_pc_t_kernel(tc, xy_sparse, decoder, x, scale, running_activity
                 )
 
         def residual(g):
-            rstd = stats.tile([P, TILES], F32)
-            nc.vector.reciprocal(out=rstd[:], in_=deviation_of[g][:])
             z = work.tile([P, TILES, D], F32)
             z_sum = stats.tile([P, TILES], F32)
             z_of[g] = z
@@ -199,7 +202,7 @@ def tile_bdhlayer_pc_t_kernel(tc, xy_sparse, decoder, x, scale, running_activity
                 nc.vector.scalar_tensor_tensor(
                     out=z[:, j, :],
                     in0=centred_of[g][:, j, :],
-                    scalar=rstd[:, j : j + 1],
+                    scalar=rstd_of[g][:, j : j + 1],
                     in1=x_tiles[g][:, j, :],
                     op0=ALU.mult,
                     op1=ALU.add,
@@ -221,24 +224,26 @@ def tile_bdhlayer_pc_t_kernel(tc, xy_sparse, decoder, x, scale, running_activity
                 )
 
         def second_root(g):
-            deviation2 = stats.tile([P, TILES], F32)
-            deviation2_of[g] = deviation2
+            rstd2 = stats.tile([P, TILES], F32)
+            rstd2_of[g] = rstd2
             nc.scalar.activation(
-                out=deviation2[:],
+                out=rstd2[:],
                 in_=square_sum_of[g][:],
-                func=ACT.Sqrt,
+                func=ACT.Abs_reciprocal_sqrt,
                 scale=1.0 / float(D * D * D),
                 bias=eps_ln[:, 0:1],
             )
 
-        def second_inverse(g):
-            rstd2 = stats.tile([P, TILES], F32)
-            rstd2_of[g] = rstd2
-            nc.vector.reciprocal(out=rstd2[:], in_=deviation2_of[g][:])
+        def second_shift(g):
             shift = stats.tile([P, TILES], F32)
             shift_of[g] = shift
             nc.vector.scalar_tensor_tensor(
-                out=shift[:], in0=z_sum_of[g][:], scalar=-1.0 / float(D), in1=rstd2[:], op0=ALU.mult, op1=ALU.mult
+                out=shift[:],
+                in0=z_sum_of[g][:],
+                scalar=-1.0 / float(D),
+                in1=rstd2_of[g][:],
+                op0=ALU.mult,
+                op1=ALU.mult,
             )
 
         def finish(g):
@@ -253,20 +258,21 @@ def tile_bdhlayer_pc_t_kernel(tc, xy_sparse, decoder, x, scale, running_activity
                 )
             nc.sync.dma_start(out=out_groups[g], in_=result[:].rearrange("p j d -> p (j d)"))
 
-        def run(stage, g):
+        def run(stage, g, *bank):
             if 0 <= g < GROUPS:
-                stage(g)
+                stage(g, *bank)
 
         for s in range(-3, GROUPS + 1):
             run(quantise, s + 1)
             run(multiply, s + 1)
             run(turn, s + 3)
+            run(regroup, s + 2, 0)
             run(second_root, s - 1)
-            run(second_inverse, s - 1)
-            run(regroup, s + 2)
-            run(finish, s - 1)
+            run(regroup, s + 2, 1)
             run(first_moments, s)
             run(first_root, s)
+            run(second_shift, s - 1)
+            run(finish, s - 1)
             run(centre, s)
             run(residual, s)
             run(second_squares, s)

@@ -47,21 +47,22 @@ def tile_bdhlayer_pc_t_kernel(tc, xy_sparse, decoder, x, scale, running_activity
         product_pool = ctx.enter_context(tc.psum_pool(name="product", bufs=2 * BANKS))
         ctx.enter_context(tc.manual_schedule())
 
-        rows = const.tile([P, 2, D], BF16)
-        nc.vector.memset(rows[:], 0.0)
-        nc.sync.dma_start(out=rows[0:1, 0, :], in_=scale.rearrange("(o d) -> o d", o=1))
-        nc.sync.dma_start(out=rows[0:1, 1, :], in_=running_activity.rearrange("(o d) -> o d", o=1))
-        dec_raw = const.tile([P, PACK, D], BF16)
-        nc.sync.dma_start(
-            out=dec_raw[:].rearrange("p (h e) d -> p h (e d)", h=HEADS),
-            in_=decoder.rearrange("(h p e) d -> p h (e d)", h=HEADS, e=2),
-        )
         xy_tiles = []
         x_tiles = []
+        rows = const.tile([P, 2, D], BF16)
+        dec_raw = const.tile([P, PACK, D], BF16)
+        nc.vector.memset(rows[:], 0.0)
         for g in range(GROUPS):
             xy_sb = inputs.tile([P, HEADS, TILES * HEAD_DIM], BF16)
             nc.sync.dma_start(out=xy_sb[:], in_=xy_groups[g])
             xy_tiles.append(xy_sb)
+            if g == 0:
+                nc.sync.dma_start(out=rows[0:1, 0, :], in_=scale.rearrange("(o d) -> o d", o=1))
+                nc.sync.dma_start(out=rows[0:1, 1, :], in_=running_activity.rearrange("(o d) -> o d", o=1))
+                nc.sync.dma_start(
+                    out=dec_raw[:].rearrange("p (h e) d -> p h (e d)", h=HEADS),
+                    in_=decoder.rearrange("(h p e) d -> p h (e d)", h=HEADS, e=2),
+                )
             x_sb = inputs.tile([P, TILES, D], BF16)
             nc.sync.dma_start(out=x_sb[:].rearrange("p j d -> p (j d)"), in_=x_groups[g])
             x_tiles.append(x_sb)
@@ -74,42 +75,44 @@ def tile_bdhlayer_pc_t_kernel(tc, xy_sparse, decoder, x, scale, running_activity
         nc.vector.memset(eps_ln[:], EPS_LN)
         eps_activity = const.tile([P, 1], F32)
         nc.vector.memset(eps_activity[:], EPS_ACTIVITY / TARGET_ACTIVITY)
-
-        dec_grouped = const.tile([P, D, PACK], BF16, align_bytes=64)
-        nc.vector.tensor_copy(out=dec_grouped[:], in_=dec_raw[:].rearrange("p t d -> p d t"))
         dec_codes = const.tile([P, D], U32, align_bytes=64)
         dec_scales = const.tile([P, D], U8, align_bytes=64)
-        nc.vector.quantize_mx(
-            out=dec_codes[:].bitcast(FP8X4),
-            scales=dec_scales[:],
-            in_=dec_grouped[:].rearrange("p d t -> p (d t)"),
-        )
-
-        spread = product_pool.tile([P, BANK_TILES, D], F32, tag="product")
-        nc.tensor.matmul(
-            spread[:].rearrange("p a d -> p (a d)"),
-            lhsT=ones[:],
-            rhs=rows[:].rearrange("p a d -> p (a d)"),
-            start=True,
-            stop=True,
-        )
-        regulation = const.tile([P, D], F32)
-        nc.scalar.activation(
-            out=regulation[:],
-            in_=spread[:, 1, :],
-            func=ACT.Abs_reciprocal_sqrt,
-            scale=1.0 / TARGET_ACTIVITY,
-            bias=eps_activity[:, 0:1],
-        )
         gain = const.tile([P, D], F32)
-        nc.vector.tensor_tensor(out=gain[:], in0=regulation[:], in1=spread[:, 0, :], op=ALU.mult)
+
+        def quantise_decoder():
+            dec_grouped = const.tile([P, D, PACK], BF16, align_bytes=64)
+            nc.vector.tensor_copy(out=dec_grouped[:], in_=dec_raw[:].rearrange("p t d -> p d t"))
+            nc.vector.quantize_mx(
+                out=dec_codes[:].bitcast(FP8X4),
+                scales=dec_scales[:],
+                in_=dec_grouped[:].rearrange("p d t -> p (d t)"),
+            )
+
+        def make_gain():
+            spread = product_pool.tile([P, BANK_TILES, D], F32, tag="product")
+            nc.tensor.matmul(
+                spread[:].rearrange("p a d -> p (a d)"),
+                lhsT=ones[:],
+                rhs=rows[:].rearrange("p a d -> p (a d)"),
+                start=True,
+                stop=True,
+            )
+            regulation = const.tile([P, D], F32)
+            nc.scalar.activation(
+                out=regulation[:],
+                in_=spread[:, 1, :],
+                func=ACT.Abs_reciprocal_sqrt,
+                scale=1.0 / TARGET_ACTIVITY,
+                bias=eps_activity[:, 0:1],
+            )
+            nc.vector.tensor_tensor(out=gain[:], in0=regulation[:], in1=spread[:, 0, :], op=ALU.mult)
 
         turned_of = {}
         grouped_of = {}
         codes_of = {}
         scales_of = {}
         products_of = {}
-        mean_var_of = {}
+        moments_of = {}
         rstd_of = {}
         centred_of = {}
         z_of = {}
@@ -151,6 +154,7 @@ def tile_bdhlayer_pc_t_kernel(tc, xy_sparse, decoder, x, scale, running_activity
             products_of[g] = []
             for b in range(BANKS):
                 product = product_pool.tile([P, BANK_TILES, D], F32)
+                products_of[g].append(product)
                 for a in range(BANK_TILES):
                     tokens = slice(P * a, P * (a + 1))
                     nc.tensor.matmul_mx(
@@ -162,22 +166,25 @@ def tile_bdhlayer_pc_t_kernel(tc, xy_sparse, decoder, x, scale, running_activity
                         start=True,
                         stop=True,
                     )
-                    products_of[g].append(product[:, a, :])
 
         def first_moments(g):
-            moments = stats.tile([P, TILES, 6], F32)
-            mean_var = stats.tile([P, TILES, 2], F32)
-            mean_var_of[g] = mean_var
-            for j in range(TILES):
-                nc.vector.bn_stats(out=moments[:, j, :], in_=products_of[g][j])
-            for j in range(TILES):
-                nc.vector.bn_aggr(out=mean_var[:, j, :], in_=moments[:, j, :])
+            moments = stats.tile([P, TILES, 3], F32)
+            moments_of[g] = moments
+            for b in range(BANKS):
+                nc.vector.bn_stats(
+                    out=moments[:, BANK_TILES * b : BANK_TILES * (b + 1), :].rearrange("p a m -> p (a m)"),
+                    in_=products_of[g][b][:].rearrange("p a d -> p d a"),
+                )
 
         def first_root(g):
             rstd = stats.tile([P, TILES], F32)
             rstd_of[g] = rstd
             nc.scalar.activation(
-                out=rstd[:], in_=mean_var_of[g][:, :, 1], func=ACT.Abs_reciprocal_sqrt, bias=eps_ln[:, 0:1]
+                out=rstd[:],
+                in_=moments_of[g][:, :, 2],
+                func=ACT.Abs_reciprocal_sqrt,
+                scale=1.0 / float(D),
+                bias=eps_ln[:, 0:1],
             )
 
         def centre(g):
@@ -186,8 +193,8 @@ def tile_bdhlayer_pc_t_kernel(tc, xy_sparse, decoder, x, scale, running_activity
             for j in range(TILES):
                 nc.vector.scalar_tensor_tensor(
                     out=centred[:, j, :],
-                    in0=products_of[g][j],
-                    scalar=mean_var_of[g][:, j, 0:1],
+                    in0=products_of[g][j // BANK_TILES][:, j % BANK_TILES, :],
+                    scalar=moments_of[g][:, j, 1:2],
                     in1=gain[:],
                     op0=ALU.subtract,
                     op1=ALU.mult,
@@ -262,7 +269,7 @@ def tile_bdhlayer_pc_t_kernel(tc, xy_sparse, decoder, x, scale, running_activity
             if 0 <= g < GROUPS:
                 stage(g, *bank)
 
-        for s in range(-3, GROUPS + 1):
+        def step(s):
             run(quantise, s + 1)
             run(multiply, s + 1)
             run(turn, s + 3)
@@ -276,3 +283,10 @@ def tile_bdhlayer_pc_t_kernel(tc, xy_sparse, decoder, x, scale, running_activity
             run(centre, s)
             run(residual, s)
             run(second_squares, s)
+
+        first_step = -3
+        step(first_step)
+        quantise_decoder()
+        make_gain()
+        for s in range(first_step + 1, GROUPS + 1):
+            step(s)

@@ -34,7 +34,7 @@ def tile_bdhlayer_pc_t_kernel(tc, xy_sparse, decoder, x, scale, running_activity
 
     xy_groups = xy_sparse[0].rearrange("h (g p j) n -> g p h (j n)", p=P, j=TILES)
     x_groups = x.flatten_outer_dims().rearrange("(g p j) d -> g p (j d)", p=P, j=TILES)
-    out_groups = out.flatten_outer_dims().rearrange("(g p j) d -> g p (j d)", p=P, j=TILES)
+    out_groups = out.flatten_outer_dims().rearrange("(g p j) d -> g p j d", p=P, j=TILES)
 
     with ExitStack() as ctx:
         const = ctx.enter_context(tc.tile_pool(name="const", bufs=1))
@@ -255,28 +255,31 @@ def tile_bdhlayer_pc_t_kernel(tc, xy_sparse, decoder, x, scale, running_activity
 
         def finish(g):
             result = results.tile([P, TILES, D], F32)
-            for j in range(TILES):
-                nc.scalar.activation(
-                    out=result[:, j, :],
-                    in_=z_of[g][:, j, :],
-                    func=ACT.Identity,
-                    scale=rstd2_of[g][:, j : j + 1],
-                    bias=shift_of[g][:, j : j + 1],
-                )
-            nc.sync.dma_start(out=out_groups[g], in_=result[:].rearrange("p j d -> p (j d)"))
+            for b in range(BANKS):
+                first = BANK_TILES * b
+                pair = slice(first, first + BANK_TILES)
+                for j in range(first, first + BANK_TILES):
+                    nc.scalar.activation(
+                        out=result[:, j, :],
+                        in_=z_of[g][:, j, :],
+                        func=ACT.Identity,
+                        scale=rstd2_of[g][:, j : j + 1],
+                        bias=shift_of[g][:, j : j + 1],
+                    )
+                nc.sync.dma_start(out=out_groups[g][:, pair, :], in_=result[:, pair, :])
 
         def run(stage, g, *bank):
             if 0 <= g < GROUPS:
                 stage(g, *bank)
 
         def step(s):
+            run(first_moments, s)
             run(quantise, s + 1)
             run(multiply, s + 1)
             run(turn, s + 3)
             run(regroup, s + 2, 0)
             run(second_root, s - 1)
             run(regroup, s + 2, 1)
-            run(first_moments, s)
             run(first_root, s)
             run(second_shift, s - 1)
             run(finish, s - 1)

@@ -45,7 +45,6 @@ def tile_bdhlayer_pc_t_kernel(tc, xy_sparse, decoder, x, scale, running_activity
         stats = ctx.enter_context(tc.tile_pool(name="stats", bufs=3))
         turned_pool = ctx.enter_context(tc.psum_pool(name="turned", bufs=2 * BANKS))
         product_pool = ctx.enter_context(tc.psum_pool(name="product", bufs=2 * BANKS))
-        ctx.enter_context(tc.manual_schedule())
 
         xy_tiles = []
         x_tiles = []

from contextlib import ExitStack

import concourse.masks as masks
import concourse.mybir as mybir

F32 = mybir.dt.float32
BF16 = mybir.dt.bfloat16
U32 = mybir.dt.uint32
U8 = mybir.dt.uint8
FP8X4 = mybir.dt.float8_e4m3fn_x4
ALU = mybir.AluOpType
ACT = mybir.ActivationFunctionType

P = 128
HEADS = 2
HEAD_DIM = 256
K = HEADS * HEAD_DIM
PACK = 4
D = 256
T = 8192
TILES = 4
BANK_TILES = 2
BANKS = TILES // BANK_TILES
GROUPS = T // (P * TILES)
EPS_LN = 1e-5
EPS_ACTIVITY = 1e-6
TARGET_ACTIVITY = 0.1

FLOPS = 2 * T * K * D


def tile_bdhlayer_pc_t_kernel(tc, xy_sparse, decoder, x, scale, running_activity, out):
    nc = tc.nc

    xy_groups = xy_sparse[0].rearrange("h (g p j) n -> g p h (j n)", p=P, j=TILES)
    x_groups = x.flatten_outer_dims().rearrange("(g p j) d -> g p (j d)", p=P, j=TILES)
    out_groups = out.flatten_outer_dims().rearrange("(g p j) d -> g p j d", p=P, j=TILES)

    with ExitStack() as ctx:
        const = ctx.enter_context(tc.tile_pool(name="const", bufs=1))
        inputs = ctx.enter_context(tc.tile_pool(name="inputs", bufs=GROUPS))
        quant = ctx.enter_context(tc.tile_pool(name="quant", bufs=2))
        work = ctx.enter_context(tc.tile_pool(name="work", bufs=3))
        results = ctx.enter_context(tc.tile_pool(name="results", bufs=4))
        stats = ctx.enter_context(tc.tile_pool(name="stats", bufs=3))
        turned_pool = ctx.enter_context(tc.psum_pool(name="turned", bufs=2 * BANKS))
        product_pool = ctx.enter_context(tc.psum_pool(name="product", bufs=2 * BANKS))

        xy_tiles = []
        x_tiles = []
        rows = const.tile([P, 2, D], BF16)
        dec_raw = const.tile([P, PACK, D], BF16)
        nc.vector.memset(rows[:], 0.0)
        for g in range(GROUPS):
            xy_sb = inputs.tile([P, HEADS, TILES * HEAD_DIM], BF16)
            nc.sync.dma_start(out=xy_sb[:], in_=xy_groups[g])
            xy_tiles.append(xy_sb)
            if g == 0:
                nc.sync.dma_start(out=rows[0:1, 0, :], in_=scale.rearrange("(o d) -> o d", o=1))
                nc.sync.dma_start(out=rows[0:1, 1, :], in_=running_activity.rearrange("(o d) -> o d", o=1))
                nc.sync.dma_start(
                    out=dec_raw[:].rearrange("p (h e) d -> p h (e d)", h=HEADS),
                    in_=decoder.rearrange("(h p e) d -> p h (e d)", h=HEADS, e=2),
                )
            x_sb = inputs.tile([P, TILES, D], BF16)
            nc.sync.dma_start(out=x_sb[:].rearrange("p j d -> p (j d)"), in_=x_groups[g])
            x_tiles.append(x_sb)

        ident = const.tile([P, P], F32)
        masks.make_identity(nc, ident[:])
        ones = const.tile([P, P], BF16)
        nc.vector.memset(ones[:], 1.0)
        eps_ln = const.tile([P, 1], F32)
        nc.vector.memset(eps_ln[:], EPS_LN)
        eps_activity = const.tile([P, 1], F32)
        nc.vector.memset(eps_activity[:], EPS_ACTIVITY / TARGET_ACTIVITY)
        dec_codes = const.tile([P, D], U32, align_bytes=64)
        dec_scales = const.tile([P, D], U8, align_bytes=64)
        gain = const.tile([P, D], F32)

        def quantise_decoder():
            dec_grouped = const.tile([P, D, PACK], BF16, align_bytes=64)
            nc.vector.tensor_copy(out=dec_grouped[:], in_=dec_raw[:].rearrange("p t d -> p d t"))
            nc.vector.quantize_mx(
                out=dec_codes[:].bitcast(FP8X4),
                scales=dec_scales[:],
                in_=dec_grouped[:].rearrange("p d t -> p (d t)"),
            )

        def make_gain():
            spread = product_pool.tile([P, BANK_TILES, D], F32, tag="product")
            nc.tensor.matmul(
                spread[:].rearrange("p a d -> p (a d)"),
                lhsT=ones[:],
                rhs=rows[:].rearrange("p a d -> p (a d)"),
                start=True,
                stop=True,
            )
            regulation = const.tile([P, D], F32)
            nc.scalar.activation(
                out=regulation[:],
                in_=spread[:, 1, :],
                func=ACT.Abs_reciprocal_sqrt,
                scale=1.0 / TARGET_ACTIVITY,
                bias=eps_activity[:, 0:1],
            )
            nc.vector.tensor_tensor(out=gain[:], in0=regulation[:], in1=spread[:, 0, :], op=ALU.mult)

        turned_of = {}
        grouped_of = {}
        codes_of = {}
        scales_of = {}
        products_of = {}
        moments_of = {}
        rstd_of = {}
        centred_of = {}
        z_of = {}
        z_sum_of = {}
        square_sum_of = {}
        rstd2_of = {}
        shift_of = {}

        def turn(g):
            xy_words = xy_tiles[g][:].bitcast(F32).rearrange("p h (j w) -> p h j w", j=TILES)
            turned_of[g] = []
            for b in range(BANKS):
                turned = turned_pool.tile([P, BANK_TILES, HEADS, P], F32)
                turned_of[g].append(turned)
                for a in range(BANK_TILES):
                    for h in range(HEADS):
                        nc.tensor.transpose(turned[:, a, h, :], xy_words[:, h, BANK_TILES * b + a, :], ident[:])

        def regroup(g, b):
            if b == 0:
                grouped = quant.tile([P, BANKS, BANK_TILES * K], BF16, align_bytes=64)
                grouped_of[g] = grouped
            nc.scalar.copy(
                out=grouped_of[g][:, b, :].bitcast(F32).rearrange("p (a t h) -> p a t h", a=BANK_TILES, h=HEADS),
                in_=turned_of[g][b][:].rearrange("p a h t -> p a t h"),
            )

        def quantise(g):
            codes = quant.tile([P, BANKS, BANK_TILES * P], U32, align_bytes=64)
            scales = quant.tile([P, BANKS, BANK_TILES * P], U8, align_bytes=64)
            codes_of[g] = codes
            scales_of[g] = scales
            for b in range(BANKS):
                nc.vector.quantize_mx(
                    out=codes[:, b, :].bitcast(FP8X4), scales=scales[:, b, :], in_=grouped_of[g][:, b, :]
                )

        def multiply(g):
            products_of[g] = []
            for b in range(BANKS):
                product = product_pool.tile([P, BANK_TILES, D], F32)
                products_of[g].append(product)
                for a in range(BANK_TILES):
                    tokens = slice(P * a, P * (a + 1))
                    nc.tensor.matmul_mx(
                        out=product[:, a, :],
                        lhsT=codes_of[g][:, b, tokens].bitcast(FP8X4),
                        lhsT_scale=scales_of[g][:, b, tokens],
                        rhs=dec_codes[:].bitcast(FP8X4),
                        rhs_scale=dec_scales[:],
                        start=True,
                        stop=True,
                    )

        def first_moments(g):
            moments = stats.tile([P, TILES, 3], F32)
            moments_of[g] = moments
            for b in range(BANKS):
                nc.vector.bn_stats(
                    out=moments[:, BANK_TILES * b : BANK_TILES * (b + 1), :].rearrange("p a m -> p (a m)"),
                    in_=products_of[g][b][:].rearrange("p a d -> p d a"),
                )

        def first_root(g):
            rstd = stats.tile([P, TILES], F32)
            rstd_of[g] = rstd
            nc.scalar.activation(
                out=rstd[:],
                in_=moments_of[g][:, :, 2],
                func=ACT.Abs_reciprocal_sqrt,
                scale=1.0 / float(D),
                bias=eps_ln[:, 0:1],
            )

        def centre(g):
            centred = work.tile([P, TILES, D], F32)
            centred_of[g] = centred
            for j in range(TILES):
                nc.vector.scalar_tensor_tensor(
                    out=centred[:, j, :],
                    in0=products_of[g][j // BANK_TILES][:, j % BANK_TILES, :],
                    scalar=moments_of[g][:, j, 1:2],
                    in1=gain[:],
                    op0=ALU.subtract,
                    op1=ALU.mult,
                )

        def residual(g):
            z = work.tile([P, TILES, D], F32)
            z_sum = stats.tile([P, TILES], F32)
            z_of[g] = z
            z_sum_of[g] = z_sum
            for j in range(TILES):
                nc.vector.scalar_tensor_tensor(
                    out=z[:, j, :],
                    in0=centred_of[g][:, j, :],
                    scalar=rstd_of[g][:, j : j + 1],
                    in1=x_tiles[g][:, j, :],
                    op0=ALU.mult,
                    op1=ALU.add,
                    accum_out=z_sum[:, j : j + 1],
                )

        def second_squares(g):
            squares = work.tile([P, TILES, D], BF16)
            square_sum = stats.tile([P, TILES], F32)
            square_sum_of[g] = square_sum
            for j in range(TILES):
                nc.scalar.activation(
                    out=squares[:, j, :],
                    in_=z_of[g][:, j, :],
                    func=ACT.Square,
                    scale=-float(D),
                    bias=z_sum_of[g][:, j : j + 1],
                    accum_out=square_sum[:, j : j + 1],
                )

        def second_root(g):
            rstd2 = stats.tile([P, TILES], F32)
            rstd2_of[g] = rstd2
            nc.scalar.activation(
                out=rstd2[:],
                in_=square_sum_of[g][:],
                func=ACT.Abs_reciprocal_sqrt,
                scale=1.0 / float(D * D * D),
                bias=eps_ln[:, 0:1],
            )

        def second_shift(g):
            shift = stats.tile([P, TILES], F32)
            shift_of[g] = shift
            nc.vector.scalar_tensor_tensor(
                out=shift[:],
                in0=z_sum_of[g][:],
                scalar=-1.0 / float(D),
                in1=rstd2_of[g][:],
                op0=ALU.mult,
                op1=ALU.mult,
            )

        def finish(g):
            result = results.tile([P, TILES, D], F32)
            for b in range(BANKS):
                first = BANK_TILES * b
                pair = slice(first, first + BANK_TILES)
                for j in range(first, first + BANK_TILES):
                    nc.scalar.activation(
                        out=result[:, j, :],
                        in_=z_of[g][:, j, :],
                        func=ACT.Identity,
                        scale=rstd2_of[g][:, j : j + 1],
                        bias=shift_of[g][:, j : j + 1],
                    )
                nc.sync.dma_start(out=out_groups[g][:, pair, :], in_=result[:, pair, :])

        def run(stage, g, *bank):
            if 0 <= g < GROUPS:
                stage(g, *bank)

        def step(s):
            run(first_moments, s)
            run(quantise, s + 1)
            run(multiply, s + 1)
            run(turn, s + 3)
            run(regroup, s + 2, 0)
            run(second_root, s - 1)
            run(regroup, s + 2, 1)
            run(first_root, s)
            run(second_shift, s - 1)
            run(finish, s - 1)
            run(centre, s)
            run(residual, s)
            run(second_squares, s)

        first_step = -3
        step(first_step)
        quantise_decoder()
        make_gain()
        for s in range(first_step + 1, GROUPS + 1):
            step(s)
